import numpy as np
import ml_dtypes


def mxq(x, axis, fmt="e4m3"):
    dtype, down = {"e4m3": (ml_dtypes.float8_e4m3fn, 7), "e5m2": (ml_dtypes.float8_e5m2, 14)}[fmt]
    v = np.moveaxis(np.asarray(x, np.float32).astype(ml_dtypes.bfloat16).astype(np.float64), axis, -1)
    blocks = v.reshape(v.shape[:-1] + (-1, 32))
    amax = np.abs(blocks).max(-1, keepdims=True)
    byte = np.maximum(np.where(amax > 0, np.frexp(amax)[1] - 1 + 127, 0) - down, 1)
    scale = np.exp2(byte - 127.0)
    codes = (blocks / scale).astype(np.float32).astype(dtype).astype(np.float64)
    return np.moveaxis((codes * scale).reshape(v.shape), -1, axis)


WIDE = False


def mx_kscale(k):
    if not WIDE:
        return np.ones(k)
    levels = np.array([10, -10, 5, -5, 0])
    a = np.random.permutation(np.resize(levels, k // 512 * 4)).reshape(k // 512, 4)
    idx = np.arange(k)
    return np.exp2(a[idx // 512, idx % 128 // 32])


BF16 = ml_dtypes.bfloat16


def bf(x):
    return np.asarray(x, np.float32).astype(BF16)


def f64(x):
    return np.asarray(x).astype(np.float64)


B, C_IN, H, W, C_OUT = 2, 16384, 16, 16, 256


def _box_sum(x):
    b, h, w, c = x.shape
    xp = np.pad(x, ((0, 0), (1, 1), (1, 1), (0, 0)))
    out = np.zeros_like(x)
    for i in range(3):
        for j in range(3):
            out = out + xp[:, i:i + h, j:j + w, :]
    return out


def setup_inputs():
    s = mx_kscale(C_IN)
    return {"x": bf(np.random.standard_normal((B, C_IN, H, W)) * s[None, :, None, None]),
            "weight": bf(np.random.standard_normal((1, C_IN, C_OUT)) * 3.0 / np.sqrt(C_IN) / s[None, :, None])}


def reference(x, weight):
    x = f64(x)
    weight = f64(weight)
    b, c, h, w = x.shape
    o = weight.shape[-1]
    x1 = np.transpose(x, (0, 2, 3, 1))
    xw = mxq(x1, 3, "e4m3") @ mxq(weight[0], 0, "e4m3")
    deg = _box_sum(np.ones((1, h, w, 1)))
    dinv = 1.0 / np.sqrt(deg)
    y = dinv * _box_sum(dinv * xw)
    return np.transpose(y, (0, 3, 1, 2)).reshape(b, o, w, h)

@@ -1,0 +1,155 @@
+import math
+
+import concourse.mybir as mybir
+
+BF16 = mybir.dt.bfloat16
+F32 = mybir.dt.float32
+U32 = mybir.dt.uint32
+U8 = mybir.dt.uint8
+FP8X4 = mybir.dt.float8_e4m3fn_x4
+
+P = 128
+PACK = 4
+K_PASS = P * PACK
+BATCH = 2
+C_IN = 16384
+C_OUT = 256
+GRID = 16
+COLS = 256
+PASSES = C_IN // K_PASS
+STEP_PASSES = 2
+STEPS = PASSES // STEP_PASSES
+M_TILES = C_OUT // P
+RUN = 4
+
+FLOPS = 2 * BATCH * GRID * GRID * C_IN * C_OUT
+
+
+def quantise_step(nc, raw_pool, grouped_pool, rows, codes, scales):
+    raw = raw_pool.tile([P, STEP_PASSES, PACK, COLS], BF16)
+    nc.sync.dma_start(out=raw[:].rearrange("p c j w -> p c (j w)"), in_=rows)
+
+    grouped = grouped_pool.tile([P, STEP_PASSES, COLS, PACK], BF16, align_bytes=64)
+    nc.vector.tensor_copy(
+        out=grouped[:, 0, :, :].rearrange("p (g i) j -> p g j i", i=RUN),
+        in_=raw[:, 0, :, :].rearrange("p j (g i) -> p g j i", i=RUN),
+    )
+    nc.scalar.copy(
+        out=grouped[:, 1, :, :].rearrange("p (g i) j -> p g j i", i=RUN),
+        in_=raw[:, 1, :, :].rearrange("p j (g i) -> p g j i", i=RUN),
+    )
+    nc.vector.quantize_mx(
+        out=codes.bitcast(FP8X4),
+        scales=scales,
+        in_=grouped[:].rearrange("p c w j -> p (c w j)"),
+    )
+
+
+def window_sums(nc, work, dinv, padded_cols, padded_rows, acc, out_b):
+    pair_j = work.tile([P, M_TILES, GRID, GRID], F32)
+    pair_i = work.tile([P, M_TILES, GRID, GRID], F32)
+    box = work.tile([P, M_TILES, GRID, GRID], F32)
+    result = work.tile([P, M_TILES, GRID, GRID], F32)
+    for m in range(M_TILES):
+        nc.vector.tensor_mul(
+            out=padded_cols[:, m, :, 1 : GRID + 1],
+            in0=acc[m][:].rearrange("p (i j) -> p i j", j=GRID),
+            in1=dinv[:],
+        )
+    for m in range(M_TILES):
+        nc.vector.tensor_add(
+            out=pair_j[:, m, :, :],
+            in0=padded_cols[:, m, :, 0:GRID],
+            in1=padded_cols[:, m, :, 1 : GRID + 1],
+        )
+    for m in range(M_TILES):
+        nc.vector.tensor_add(
+            out=padded_rows[:, m, 1 : GRID + 1, :],
+            in0=pair_j[:, m, :, :],
+            in1=padded_cols[:, m, :, 2 : GRID + 2],
+        )
+    for m in range(M_TILES):
+        nc.vector.tensor_add(
+            out=pair_i[:, m, :, :],
+            in0=padded_rows[:, m, 0:GRID, :],
+            in1=padded_rows[:, m, 1 : GRID + 1, :],
+        )
+    for m in range(M_TILES):
+        nc.vector.tensor_add(
+            out=box[:, m, :, :],
+            in0=pair_i[:, m, :, :],
+            in1=padded_rows[:, m, 2 : GRID + 2, :],
+        )
+    for m in range(M_TILES):
+        nc.vector.tensor_mul(out=result[:, m, :, :], in0=box[:, m, :, :], in1=dinv[:])
+        nc.sync.dma_start(
+            out=out_b[:, m, :], in_=result[:, m, :, :].rearrange("p i j -> p (i j)")
+        )
+
+
+def tile_gcn_layer_k_kernel(tc, x, weight, out):
+    nc = tc.nc
+    x_rows = x.rearrange("b (c p j) h w -> b p c (j h w)", p=P, j=PACK)
+    w_rows = weight.rearrange("one (c p j) o -> p (one c) (j o)", p=P, j=PACK)
+    out_view = out.rearrange("b (m o) i j -> b o m (i j)", o=P)
+
+    with tc.tile_pool(name="keep", bufs=1) as keep, tc.tile_pool(
+        name="raw", bufs=8
+    ) as raw_pool, tc.tile_pool(name="grouped", bufs=4) as grouped_pool, tc.tile_pool(
+        name="x_mx", bufs=4
+    ) as x_mx, tc.tile_pool(name="work", bufs=2) as work, tc.psum_pool(
+        name="psum", bufs=1
+    ) as psum:
+        dinv = keep.tile([P, GRID, GRID], F32)
+        nc.vector.memset(dinv[:], 1.0)
+        nc.vector.tensor_scalar_mul(out=dinv[:], in0=dinv[:], scalar1=1.0 / 3.0)
+        border_rows = dinv[:, 0 : GRID : GRID - 1, :]
+        nc.vector.tensor_scalar_mul(out=border_rows, in0=border_rows, scalar1=math.sqrt(1.5))
+        border_cols = dinv[:, :, 0 : GRID : GRID - 1]
+        nc.vector.tensor_scalar_mul(out=border_cols, in0=border_cols, scalar1=math.sqrt(1.5))
+
+        padded_cols = keep.tile([P, M_TILES, GRID, GRID + 2], F32)
+        nc.vector.memset(padded_cols[:], 0.0)
+        padded_rows = keep.tile([P, M_TILES, GRID + 2, GRID], F32)
+        nc.vector.memset(padded_rows[:], 0.0)
+
+        w_codes = keep.tile([P, PASSES, C_OUT], U32, align_bytes=64)
+        w_scales = keep.tile([P, PASSES, C_OUT], U8, align_bytes=64)
+
+        for b in range(BATCH):
+            acc = [psum.tile([P, COLS], F32, name="acc_%d_%d" % (b, m)) for m in range(M_TILES)]
+            for s in range(STEPS):
+                passes = slice(s * STEP_PASSES, (s + 1) * STEP_PASSES)
+                if b == 0:
+                    quantise_step(
+                        nc,
+                        raw_pool,
+                        grouped_pool,
+                        w_rows[:, passes, :],
+                        w_codes[:, passes, :].rearrange("p c o -> p (c o)"),
+                        w_scales[:, passes, :].rearrange("p c o -> p (c o)"),
+                    )
+                x_codes = x_mx.tile([P, STEP_PASSES, COLS], U32, align_bytes=64)
+                x_scales = x_mx.tile([P, STEP_PASSES, COLS], U8, align_bytes=64)
+                quantise_step(
+                    nc,
+                    raw_pool,
+                    grouped_pool,
+                    x_rows[b, :, passes, :],
+                    x_codes[:].rearrange("p c w -> p (c w)"),
+                    x_scales[:].rearrange("p c w -> p (c w)"),
+                )
+                for c in range(STEP_PASSES):
+                    k_pass = s * STEP_PASSES + c
+                    for m in range(M_TILES):
+                        o_cols = slice(m * P, (m + 1) * P)
+                        nc.tensor.matmul_mx(
+                            out=acc[m][:],
+                            lhsT=w_codes[:, k_pass, o_cols].bitcast(FP8X4),
+                            lhsT_scale=w_scales[:, k_pass, o_cols],
+                            rhs=x_codes[:, c, :].bitcast(FP8X4),
+                            rhs_scale=x_scales[:, c, :],
+                            start=(k_pass == 0),
+                            stop=(k_pass == PASSES - 1),
+                        )
+            window_sums(nc, work, dinv, padded_cols, padded_rows, acc, out_view[b])

@@ -1,5 +1,6 @@
 import math
 
+import concourse.masks as masks
 import concourse.mybir as mybir
 
 BF16 = mybir.dt.bfloat16
@@ -15,14 +16,73 @@ BATCH = 2
 C_IN = 16384
 C_OUT = 256
 GRID = 16
+PIXELS = GRID * GRID
 COLS = 256
 PASSES = C_IN // K_PASS
 STEP_PASSES = 2
 STEPS = PASSES // STEP_PASSES
+HALVES = PIXELS // P
 M_TILES = C_OUT // P
+
+FLOPS = 2 * BATCH * PIXELS * C_IN * C_OUT + 2 * BATCH * PIXELS * PIXELS * C_OUT
 RUN = 4
 
-FLOPS = 2 * BATCH * GRID * GRID * C_IN * C_OUT
+
+def build_graph(nc, keep):
+    dinv = keep.tile([P, GRID, GRID], F32)
+    nc.vector.memset(dinv[:], 1.0)
+    nc.vector.tensor_scalar_mul(out=dinv[:], in0=dinv[:], scalar1=1.0 / 3.0)
+    border_rows = dinv[:, 0 : GRID : GRID - 1, :]
+    nc.vector.tensor_scalar_mul(out=border_rows, in0=border_rows, scalar1=math.sqrt(1.5))
+    border_cols = dinv[:, :, 0 : GRID : GRID - 1]
+    nc.vector.tensor_scalar_mul(out=border_cols, in0=border_cols, scalar1=math.sqrt(1.5))
+
+    one_pixel = keep.tile([P, HALVES, PIXELS], F32)
+    nc.gpsimd.memset(one_pixel[:], 0.0)
+    for h in range(HALVES):
+        masks.make_identity(nc, one_pixel[:, h, h * P : (h + 1) * P], nomemset=True)
+
+    padded_cols = keep.tile([P, HALVES, GRID, GRID + 2], F32)
+    nc.vector.memset(padded_cols[:], 0.0)
+    padded_rows = keep.tile([P, HALVES, GRID + 2, GRID], F32)
+    nc.vector.memset(padded_rows[:], 0.0)
+    pair_j = keep.tile([P, HALVES, GRID, GRID], F32)
+    pair_i = keep.tile([P, HALVES, GRID, GRID], F32)
+    box = keep.tile([P, HALVES, GRID, GRID], F32)
+    graph = keep.tile([P, HALVES, GRID, GRID], F32)
+    for h in range(HALVES):
+        nc.vector.tensor_mul(
+            out=padded_cols[:, h, :, 1 : GRID + 1],
+            in0=one_pixel[:, h, :].rearrange("p (i j) -> p i j", j=GRID),
+            in1=dinv[:],
+        )
+    for h in range(HALVES):
+        nc.vector.tensor_add(
+            out=pair_j[:, h, :, :],
+            in0=padded_cols[:, h, :, 0:GRID],
+            in1=padded_cols[:, h, :, 1 : GRID + 1],
+        )
+    for h in range(HALVES):
+        nc.vector.tensor_add(
+            out=padded_rows[:, h, 1 : GRID + 1, :],
+            in0=pair_j[:, h, :, :],
+            in1=padded_cols[:, h, :, 2 : GRID + 2],
+        )
+    for h in range(HALVES):
+        nc.vector.tensor_add(
+            out=pair_i[:, h, :, :],
+            in0=padded_rows[:, h, 0:GRID, :],
+            in1=padded_rows[:, h, 1 : GRID + 1, :],
+        )
+    for h in range(HALVES):
+        nc.vector.tensor_add(
+            out=box[:, h, :, :],
+            in0=pair_i[:, h, :, :],
+            in1=padded_rows[:, h, 2 : GRID + 2, :],
+        )
+    for h in range(HALVES):
+        nc.vector.tensor_mul(out=graph[:, h, :, :], in0=box[:, h, :, :], in1=dinv[:])
+    return graph
 
 
 def quantise_step(nc, raw_pool, grouped_pool, rows, codes, scales):
@@ -45,46 +105,25 @@ def quantise_step(nc, raw_pool, grouped_pool, rows, codes, scales):
     )
 
 
-def window_sums(nc, work, dinv, padded_cols, padded_rows, acc, out_b):
-    pair_j = work.tile([P, M_TILES, GRID, GRID], F32)
-    pair_i = work.tile([P, M_TILES, GRID, GRID], F32)
-    box = work.tile([P, M_TILES, GRID, GRID], F32)
-    result = work.tile([P, M_TILES, GRID, GRID], F32)
+def apply_graph(nc, work, psum, graph, b, acc, out_b):
+    xw = work.tile([P, HALVES, C_OUT], F32)
+    nc.vector.tensor_copy(out=xw[:, 0, :], in_=acc[0][:])
+    nc.scalar.copy(out=xw[:, 1, :], in_=acc[1][:])
+    summed = [psum.tile([P, PIXELS], F32, name="summed_%d_%d" % (b, m)) for m in range(M_TILES)]
     for m in range(M_TILES):
-        nc.vector.tensor_mul(
-            out=padded_cols[:, m, :, 1 : GRID + 1],
-            in0=acc[m][:].rearrange("p (i j) -> p i j", j=GRID),
-            in1=dinv[:],
-        )
-    for m in range(M_TILES):
-        nc.vector.tensor_add(
-            out=pair_j[:, m, :, :],
-            in0=padded_cols[:, m, :, 0:GRID],
-            in1=padded_cols[:, m, :, 1 : GRID + 1],
-        )
-    for m in range(M_TILES):
-        nc.vector.tensor_add(
-            out=padded_rows[:, m, 1 : GRID + 1, :],
-            in0=pair_j[:, m, :, :],
-            in1=padded_cols[:, m, :, 2 : GRID + 2],
-        )
-    for m in range(M_TILES):
-        nc.vector.tensor_add(
-            out=pair_i[:, m, :, :],
-            in0=padded_rows[:, m, 0:GRID, :],
-            in1=padded_rows[:, m, 1 : GRID + 1, :],
-        )
-    for m in range(M_TILES):
-        nc.vector.tensor_add(
-            out=box[:, m, :, :],
-            in0=pair_i[:, m, :, :],
-            in1=padded_rows[:, m, 2 : GRID + 2, :],
-        )
-    for m in range(M_TILES):
-        nc.vector.tensor_mul(out=result[:, m, :, :], in0=box[:, m, :, :], in1=dinv[:])
-        nc.sync.dma_start(
-            out=out_b[:, m, :], in_=result[:, m, :, :].rearrange("p i j -> p (i j)")
-        )
+        for h in range(HALVES):
+            nc.tensor.matmul(
+                out=summed[m][:],
+                lhsT=xw[:, h, m * P : (m + 1) * P],
+                rhs=graph[:, h, :, :].rearrange("p i j -> p (i j)"),
+                start=(h == 0),
+                stop=(h == HALVES - 1),
+            )
+    result = work.tile([P, M_TILES, PIXELS], F32)
+    nc.vector.tensor_copy(out=result[:, 0, :], in_=summed[0][:])
+    nc.sync.dma_start(out=out_b[:, 0, :], in_=result[:, 0, :])
+    nc.scalar.copy(out=result[:, 1, :], in_=summed[1][:])
+    nc.sync.dma_start(out=out_b[:, 1, :], in_=result[:, 1, :])
 
 
 def tile_gcn_layer_k_kernel(tc, x, weight, out):
@@ -100,24 +139,13 @@ def tile_gcn_layer_k_kernel(tc, x, weight, out):
     ) as x_mx, tc.tile_pool(name="work", bufs=2) as work, tc.psum_pool(
         name="psum", bufs=1
     ) as psum:
-        dinv = keep.tile([P, GRID, GRID], F32)
-        nc.vector.memset(dinv[:], 1.0)
-        nc.vector.tensor_scalar_mul(out=dinv[:], in0=dinv[:], scalar1=1.0 / 3.0)
-        border_rows = dinv[:, 0 : GRID : GRID - 1, :]
-        nc.vector.tensor_scalar_mul(out=border_rows, in0=border_rows, scalar1=math.sqrt(1.5))
-        border_cols = dinv[:, :, 0 : GRID : GRID - 1]
-        nc.vector.tensor_scalar_mul(out=border_cols, in0=border_cols, scalar1=math.sqrt(1.5))
-
-        padded_cols = keep.tile([P, M_TILES, GRID, GRID + 2], F32)
-        nc.vector.memset(padded_cols[:], 0.0)
-        padded_rows = keep.tile([P, M_TILES, GRID + 2, GRID], F32)
-        nc.vector.memset(padded_rows[:], 0.0)
+        graph = build_graph(nc, keep)
 
         w_codes = keep.tile([P, PASSES, C_OUT], U32, align_bytes=64)
         w_scales = keep.tile([P, PASSES, C_OUT], U8, align_bytes=64)
 
         for b in range(BATCH):
-            acc = [psum.tile([P, COLS], F32, name="acc_%d_%d" % (b, m)) for m in range(M_TILES)]
+            acc = [psum.tile([P, C_OUT], F32, name="acc_%d_%d" % (b, h)) for h in range(HALVES)]
             for s in range(STEPS):
                 passes = slice(s * STEP_PASSES, (s + 1) * STEP_PASSES)
                 if b == 0:
@@ -129,8 +157,8 @@ def tile_gcn_layer_k_kernel(tc, x, weight, out):
                         w_codes[:, passes, :].rearrange("p c o -> p (c o)"),
                         w_scales[:, passes, :].rearrange("p c o -> p (c o)"),
                     )
-                x_codes = x_mx.tile([P, STEP_PASSES, COLS], U32, align_bytes=64)
-                x_scales = x_mx.tile([P, STEP_PASSES, COLS], U8, align_bytes=64)
+                x_codes = x_mx.tile([P, STEP_PASSES, PIXELS], U32, align_bytes=64)
+                x_scales = x_mx.tile([P, STEP_PASSES, PIXELS], U8, align_bytes=64)
                 quantise_step(
                     nc,
                     raw_pool,
@@ -141,15 +169,15 @@ def tile_gcn_layer_k_kernel(tc, x, weight, out):
                 )
                 for c in range(STEP_PASSES):
                     k_pass = s * STEP_PASSES + c
-                    for m in range(M_TILES):
-                        o_cols = slice(m * P, (m + 1) * P)
+                    for h in range(HALVES):
+                        pixels = slice(h * P, (h + 1) * P)
                         nc.tensor.matmul_mx(
-                            out=acc[m][:],
-                            lhsT=w_codes[:, k_pass, o_cols].bitcast(FP8X4),
-                            lhsT_scale=w_scales[:, k_pass, o_cols],
-                            rhs=x_codes[:, c, :].bitcast(FP8X4),
-                            rhs_scale=x_scales[:, c, :],
+                            out=acc[h][:],
+                            lhsT=x_codes[:, c, pixels].bitcast(FP8X4),
+                            lhsT_scale=x_scales[:, c, pixels],
+                            rhs=w_codes[:, k_pass, :].bitcast(FP8X4),
+                            rhs_scale=w_scales[:, k_pass, :],
                             start=(k_pass == 0),
                             stop=(k_pass == PASSES - 1),
                         )
-            window_sums(nc, work, dinv, padded_cols, padded_rows, acc, out_view[b])
+            apply_graph(nc, work, psum, graph, b, acc, out_view[b])

@@ -22,13 +22,20 @@ PASSES = C_IN // K_PASS
 STEP_PASSES = 2
 STEPS = PASSES // STEP_PASSES
 HALVES = PIXELS // P
+HALF_ROWS = GRID // HALVES
 M_TILES = C_OUT // P
 
 FLOPS = 2 * BATCH * PIXELS * C_IN * C_OUT + 2 * BATCH * PIXELS * PIXELS * C_OUT
 RUN = 4
+SCALAR_BOTH_EVERY = 12
+SUM_AT_STEP = 2
+LEAVE_AT_STEP = 6
 
 
 def build_graph(nc, keep):
+    one_pixel = keep.tile([P, P], F32)
+    masks.make_identity(nc, one_pixel[:])
+
     dinv = keep.tile([P, GRID, GRID], F32)
     nc.vector.memset(dinv[:], 1.0)
     nc.vector.tensor_scalar_mul(out=dinv[:], in0=dinv[:], scalar1=1.0 / 3.0)
@@ -37,24 +44,19 @@ def build_graph(nc, keep):
     border_cols = dinv[:, :, 0 : GRID : GRID - 1]
     nc.vector.tensor_scalar_mul(out=border_cols, in0=border_cols, scalar1=math.sqrt(1.5))
 
-    one_pixel = keep.tile([P, HALVES, PIXELS], F32)
-    nc.gpsimd.memset(one_pixel[:], 0.0)
-    for h in range(HALVES):
-        masks.make_identity(nc, one_pixel[:, h, h * P : (h + 1) * P], nomemset=True)
-
-    padded_cols = keep.tile([P, HALVES, GRID, GRID + 2], F32)
+    padded_cols = keep.tile([P, HALVES, HALF_ROWS, GRID + 2], F32)
     nc.vector.memset(padded_cols[:], 0.0)
     padded_rows = keep.tile([P, HALVES, GRID + 2, GRID], F32)
     nc.vector.memset(padded_rows[:], 0.0)
-    pair_j = keep.tile([P, HALVES, GRID, GRID], F32)
+    pair_j = keep.tile([P, HALVES, HALF_ROWS, GRID], F32)
     pair_i = keep.tile([P, HALVES, GRID, GRID], F32)
     box = keep.tile([P, HALVES, GRID, GRID], F32)
     graph = keep.tile([P, HALVES, GRID, GRID], F32)
     for h in range(HALVES):
         nc.vector.tensor_mul(
             out=padded_cols[:, h, :, 1 : GRID + 1],
-            in0=one_pixel[:, h, :].rearrange("p (i j) -> p i j", j=GRID),
-            in1=dinv[:],
+            in0=one_pixel[:].rearrange("p (i j) -> p i j", j=GRID),
+            in1=dinv[:, h * HALF_ROWS : (h + 1) * HALF_ROWS, :],
         )
     for h in range(HALVES):
         nc.vector.tensor_add(
@@ -64,7 +66,7 @@ def build_graph(nc, keep):
         )
     for h in range(HALVES):
         nc.vector.tensor_add(
-            out=padded_rows[:, h, 1 : GRID + 1, :],
+            out=padded_rows[:, h, 1 + h * HALF_ROWS : 1 + (h + 1) * HALF_ROWS, :],
             in0=pair_j[:, h, :, :],
             in1=padded_cols[:, h, :, 2 : GRID + 2],
         )
@@ -85,12 +87,12 @@ def build_graph(nc, keep):
     return graph
 
 
-def quantise_step(nc, raw_pool, grouped_pool, rows, codes, scales):
+def regroup_step(nc, raw_pool, grouped_pool, rows, first_copy):
     raw = raw_pool.tile([P, STEP_PASSES, PACK, COLS], BF16)
     nc.sync.dma_start(out=raw[:].rearrange("p c j w -> p c (j w)"), in_=rows)
 
     grouped = grouped_pool.tile([P, STEP_PASSES, COLS, PACK], BF16, align_bytes=64)
-    nc.vector.tensor_copy(
+    first_copy(
         out=grouped[:, 0, :, :].rearrange("p (g i) j -> p g j i", i=RUN),
         in_=raw[:, 0, :, :].rearrange("p j (g i) -> p g j i", i=RUN),
     )
@@ -98,14 +100,18 @@ def quantise_step(nc, raw_pool, grouped_pool, rows, codes, scales):
         out=grouped[:, 1, :, :].rearrange("p (g i) j -> p g j i", i=RUN),
         in_=raw[:, 1, :, :].rearrange("p j (g i) -> p g j i", i=RUN),
     )
+    return grouped
+
+
+def quantise(nc, grouped, codes, scales):
     nc.vector.quantize_mx(
-        out=codes.bitcast(FP8X4),
-        scales=scales,
+        out=codes.rearrange("p c w -> p (c w)").bitcast(FP8X4),
+        scales=scales.rearrange("p c w -> p (c w)"),
         in_=grouped[:].rearrange("p c w j -> p (c w j)"),
     )
 
 
-def apply_graph(nc, work, psum, graph, b, acc, out_b):
+def sum_windows(nc, work, psum, graph, b, acc):
     xw = work.tile([P, HALVES, C_OUT], F32)
     nc.vector.tensor_copy(out=xw[:, 0, :], in_=acc[0][:])
     nc.scalar.copy(out=xw[:, 1, :], in_=acc[1][:])
@@ -119,11 +125,14 @@ def apply_graph(nc, work, psum, graph, b, acc, out_b):
                 start=(h == 0),
                 stop=(h == HALVES - 1),
             )
+    return summed
+
+
+def leave_psum(nc, work, summed):
     result = work.tile([P, M_TILES, PIXELS], F32)
     nc.vector.tensor_copy(out=result[:, 0, :], in_=summed[0][:])
-    nc.sync.dma_start(out=out_b[:, 0, :], in_=result[:, 0, :])
     nc.scalar.copy(out=result[:, 1, :], in_=summed[1][:])
-    nc.sync.dma_start(out=out_b[:, 1, :], in_=result[:, 1, :])
+    return result
 
 
 def tile_gcn_layer_k_kernel(tc, x, weight, out):
@@ -132,52 +141,67 @@ def tile_gcn_layer_k_kernel(tc, x, weight, out):
     w_rows = weight.rearrange("one (c p j) o -> p (one c) (j o)", p=P, j=PACK)
     out_view = out.rearrange("b (m o) i j -> b o m (i j)", o=P)
 
+    stream = []
+    for s in range(STEPS):
+        stream.append((None, s))
+        stream.append((0, s))
+    for s in range(STEPS):
+        stream.append((1, s))
+
     with tc.tile_pool(name="keep", bufs=1) as keep, tc.tile_pool(
-        name="raw", bufs=8
+        name="raw", bufs=12
     ) as raw_pool, tc.tile_pool(name="grouped", bufs=4) as grouped_pool, tc.tile_pool(
         name="x_mx", bufs=4
     ) as x_mx, tc.tile_pool(name="work", bufs=2) as work, tc.psum_pool(
         name="psum", bufs=1
-    ) as psum:
+    ) as psum, tc.manual_schedule():
         graph = build_graph(nc, keep)
 
         w_codes = keep.tile([P, PASSES, C_OUT], U32, align_bytes=64)
         w_scales = keep.tile([P, PASSES, C_OUT], U8, align_bytes=64)
+        acc = [
+            [psum.tile([P, C_OUT], F32, name="acc_%d_%d" % (b, h)) for h in range(HALVES)]
+            for b in range(BATCH)
+        ]
 
-        for b in range(BATCH):
-            acc = [psum.tile([P, C_OUT], F32, name="acc_%d_%d" % (b, h)) for h in range(HALVES)]
-            for s in range(STEPS):
-                passes = slice(s * STEP_PASSES, (s + 1) * STEP_PASSES)
-                if b == 0:
-                    quantise_step(
-                        nc,
-                        raw_pool,
-                        grouped_pool,
-                        w_rows[:, passes, :],
-                        w_codes[:, passes, :].rearrange("p c o -> p (c o)"),
-                        w_scales[:, passes, :].rearrange("p c o -> p (c o)"),
+        def quantise_and_multiply(grouped, b, s):
+            passes = slice(s * STEP_PASSES, (s + 1) * STEP_PASSES)
+            if b is None:
+                quantise(nc, grouped, w_codes[:, passes, :], w_scales[:, passes, :])
+                return
+            x_codes = x_mx.tile([P, STEP_PASSES, PIXELS], U32, align_bytes=64)
+            x_scales = x_mx.tile([P, STEP_PASSES, PIXELS], U8, align_bytes=64)
+            quantise(nc, grouped, x_codes[:], x_scales[:])
+            for c in range(STEP_PASSES):
+                k_pass = s * STEP_PASSES + c
+                for h in range(HALVES):
+                    pixels = slice(h * P, (h + 1) * P)
+                    nc.tensor.matmul_mx(
+                        out=acc[b][h][:],
+                        lhsT=x_codes[:, c, pixels].bitcast(FP8X4),
+                        lhsT_scale=x_scales[:, c, pixels],
+                        rhs=w_codes[:, k_pass, :].bitcast(FP8X4),
+                        rhs_scale=w_scales[:, k_pass, :],
+                        start=(k_pass == 0),
+                        stop=(k_pass == PASSES - 1),
                     )
-                x_codes = x_mx.tile([P, STEP_PASSES, PIXELS], U32, align_bytes=64)
-                x_scales = x_mx.tile([P, STEP_PASSES, PIXELS], U8, align_bytes=64)
-                quantise_step(
-                    nc,
-                    raw_pool,
-                    grouped_pool,
-                    x_rows[b, :, passes, :],
-                    x_codes[:].rearrange("p c w -> p (c w)"),
-                    x_scales[:].rearrange("p c w -> p (c w)"),
-                )
-                for c in range(STEP_PASSES):
-                    k_pass = s * STEP_PASSES + c
-                    for h in range(HALVES):
-                        pixels = slice(h * P, (h + 1) * P)
-                        nc.tensor.matmul_mx(
-                            out=acc[h][:],
-                            lhsT=x_codes[:, c, pixels].bitcast(FP8X4),
-                            lhsT_scale=x_scales[:, c, pixels],
-                            rhs=w_codes[:, k_pass, :].bitcast(FP8X4),
-                            rhs_scale=w_scales[:, k_pass, :],
-                            start=(k_pass == 0),
-                            stop=(k_pass == PASSES - 1),
-                        )
-            apply_graph(nc, work, psum, graph, b, acc, out_view[b])
+
+        regrouped = None
+        for n, (b, s) in enumerate(stream):
+            passes = slice(s * STEP_PASSES, (s + 1) * STEP_PASSES)
+            rows = w_rows[:, passes, :] if b is None else x_rows[b, :, passes, :]
+            first_copy = nc.scalar.copy if n % SCALAR_BOTH_EVERY == 0 else nc.vector.tensor_copy
+            grouped = regroup_step(nc, raw_pool, grouped_pool, rows, first_copy)
+            if regrouped is not None:
+                quantise_and_multiply(*regrouped)
+            regrouped = (grouped, b, s)
+            if b == 1 and s == SUM_AT_STEP:
+                summed_0 = sum_windows(nc, work, psum, graph, 0, acc[0])
+            if b == 1 and s == LEAVE_AT_STEP:
+                result_0 = leave_psum(nc, work, summed_0)
+        quantise_and_multiply(*regrouped)
+        result_1 = leave_psum(nc, work, sum_windows(nc, work, psum, graph, 1, acc[1]))
+
+        for b, result in enumerate((result_0, result_1)):
+            for m in range(M_TILES):
+                nc.sync.dma_start(out=out_view[b, :, m, :], in_=result[:, m, :])

@@ -27,7 +27,6 @@ M_TILES = C_OUT // P
 
 FLOPS = 2 * BATCH * PIXELS * C_IN * C_OUT + 2 * BATCH * PIXELS * PIXELS * C_OUT
 RUN = 4
-SCALAR_BOTH_EVERY = 12
 SUM_AT_STEP = 2
 LEAVE_AT_STEP = 6
 
@@ -36,63 +35,50 @@ def build_graph(nc, keep):
     one_pixel = keep.tile([P, P], F32)
     masks.make_identity(nc, one_pixel[:])
 
-    dinv = keep.tile([P, GRID, GRID], F32)
-    nc.vector.memset(dinv[:], 1.0)
-    nc.vector.tensor_scalar_mul(out=dinv[:], in0=dinv[:], scalar1=1.0 / 3.0)
-    border_rows = dinv[:, 0 : GRID : GRID - 1, :]
-    nc.vector.tensor_scalar_mul(out=border_rows, in0=border_rows, scalar1=math.sqrt(1.5))
-    border_cols = dinv[:, :, 0 : GRID : GRID - 1]
-    nc.vector.tensor_scalar_mul(out=border_cols, in0=border_cols, scalar1=math.sqrt(1.5))
+    s = keep.tile([P, GRID], F32)
+    nc.vector.memset(s[:], 1.0)
+    nc.vector.tensor_scalar_mul(out=s[:], in0=s[:], scalar1=1.0 / math.sqrt(3.0))
+    ends = s[:, 0 : GRID : GRID - 1]
+    nc.vector.tensor_scalar_mul(out=ends, in0=ends, scalar1=math.sqrt(1.5))
+    s_all = s[:].unsqueeze(1).to_broadcast([P, 1 + HALVES, GRID])
 
-    padded_cols = keep.tile([P, HALVES, HALF_ROWS, GRID + 2], F32)
-    nc.vector.memset(padded_cols[:], 0.0)
-    padded_rows = keep.tile([P, HALVES, GRID + 2, GRID], F32)
-    nc.vector.memset(padded_rows[:], 0.0)
-    pair_j = keep.tile([P, HALVES, HALF_ROWS, GRID], F32)
-    pair_i = keep.tile([P, HALVES, GRID, GRID], F32)
-    box = keep.tile([P, HALVES, GRID, GRID], F32)
+    padded = keep.tile([P, 1 + HALVES, GRID + 2], F32)
+    nc.vector.memset(padded[:], 0.0)
+    nc.vector.tensor_reduce(
+        out=padded[:, 0, 1 : GRID + 1],
+        in_=one_pixel[:].rearrange("p (i j) -> p j i", j=GRID),
+        axis=mybir.AxisListType.X,
+        op=mybir.AluOpType.add,
+    )
+    for h in range(HALVES):
+        nc.vector.tensor_reduce(
+            out=padded[:, 1 + h, 1 + h * HALF_ROWS : 1 + (h + 1) * HALF_ROWS],
+            in_=one_pixel[:].rearrange("p (i j) -> p i j", j=GRID),
+            axis=mybir.AxisListType.X,
+            op=mybir.AluOpType.add,
+        )
+    centre = padded[:, :, 1 : GRID + 1]
+    nc.vector.tensor_mul(out=centre, in0=centre, in1=s_all)
+    factors = keep.tile([P, 1 + HALVES, GRID], F32)
+    nc.vector.tensor_add(out=factors[:], in0=padded[:, :, 0:GRID], in1=centre)
+    nc.vector.tensor_add(out=factors[:], in0=factors[:], in1=padded[:, :, 2 : GRID + 2])
+    nc.vector.tensor_mul(out=factors[:], in0=factors[:], in1=s_all)
+
     graph = keep.tile([P, HALVES, GRID, GRID], F32)
-    for h in range(HALVES):
-        nc.vector.tensor_mul(
-            out=padded_cols[:, h, :, 1 : GRID + 1],
-            in0=one_pixel[:].rearrange("p (i j) -> p i j", j=GRID),
-            in1=dinv[:, h * HALF_ROWS : (h + 1) * HALF_ROWS, :],
-        )
-    for h in range(HALVES):
-        nc.vector.tensor_add(
-            out=pair_j[:, h, :, :],
-            in0=padded_cols[:, h, :, 0:GRID],
-            in1=padded_cols[:, h, :, 1 : GRID + 1],
-        )
-    for h in range(HALVES):
-        nc.vector.tensor_add(
-            out=padded_rows[:, h, 1 + h * HALF_ROWS : 1 + (h + 1) * HALF_ROWS, :],
-            in0=pair_j[:, h, :, :],
-            in1=padded_cols[:, h, :, 2 : GRID + 2],
-        )
-    for h in range(HALVES):
-        nc.vector.tensor_add(
-            out=pair_i[:, h, :, :],
-            in0=padded_rows[:, h, 0:GRID, :],
-            in1=padded_rows[:, h, 1 : GRID + 1, :],
-        )
-    for h in range(HALVES):
-        nc.vector.tensor_add(
-            out=box[:, h, :, :],
-            in0=pair_i[:, h, :, :],
-            in1=padded_rows[:, h, 2 : GRID + 2, :],
-        )
-    for h in range(HALVES):
-        nc.vector.tensor_mul(out=graph[:, h, :, :], in0=box[:, h, :, :], in1=dinv[:])
+    nc.vector.tensor_mul(
+        out=graph[:],
+        in0=factors[:, 1 : 1 + HALVES, :].unsqueeze(3).to_broadcast([P, HALVES, GRID, GRID]),
+        in1=factors[:, 0:1, :].unsqueeze(1).to_broadcast([P, HALVES, GRID, GRID]),
+    )
     return graph
 
 
-def regroup_step(nc, raw_pool, grouped_pool, rows, first_copy):
+def regroup_step(nc, raw_pool, grouped_pool, rows):
     raw = raw_pool.tile([P, STEP_PASSES, PACK, COLS], BF16)
     nc.sync.dma_start(out=raw[:].rearrange("p c j w -> p c (j w)"), in_=rows)
 
     grouped = grouped_pool.tile([P, STEP_PASSES, COLS, PACK], BF16, align_bytes=64)
-    first_copy(
+    nc.vector.tensor_copy(
         out=grouped[:, 0, :, :].rearrange("p (g i) j -> p g j i", i=RUN),
         in_=raw[:, 0, :, :].rearrange("p j (g i) -> p g j i", i=RUN),
     )
@@ -190,8 +176,7 @@ def tile_gcn_layer_k_kernel(tc, x, weight, out):
         for n, (b, s) in enumerate(stream):
             passes = slice(s * STEP_PASSES, (s + 1) * STEP_PASSES)
             rows = w_rows[:, passes, :] if b is None else x_rows[b, :, passes, :]
-            first_copy = nc.scalar.copy if n % SCALAR_BOTH_EVERY == 0 else nc.vector.tensor_copy
-            grouped = regroup_step(nc, raw_pool, grouped_pool, rows, first_copy)
+            grouped = regroup_step(nc, raw_pool, grouped_pool, rows)
             if regrouped is not None:
                 quantise_and_multiply(*regrouped)
             regrouped = (grouped, b, s)

@@ -20,6 +20,7 @@ PIXELS = GRID * GRID
 COLS = 256
 PASSES = C_IN // K_PASS
 STEP_PASSES = 2
+LOAD_PASSES = 4
 STEPS = PASSES // STEP_PASSES
 HALVES = PIXELS // P
 HALF_ROWS = GRID // HALVES
@@ -73,19 +74,20 @@ def build_graph(nc, keep):
     return graph
 
 
-def regroup_step(nc, raw_pool, grouped_pool, rows):
-    raw = raw_pool.tile([P, STEP_PASSES, PACK, COLS], BF16)
-    nc.sync.dma_start(out=raw[:].rearrange("p c j w -> p c (j w)"), in_=rows)
+def load_passes(nc, raw_pools, rows, passes):
+    count = passes.stop - passes.start
+    raw = raw_pools[count].tile([P, count, PACK, COLS], BF16, name="raw_%d" % count)
+    nc.sync.dma_start(out=raw[:].rearrange("p c j w -> p c (j w)"), in_=rows[:, passes, :])
+    return raw
 
+
+def regroup_step(nc, grouped_pool, raw):
     grouped = grouped_pool.tile([P, STEP_PASSES, COLS, PACK], BF16, align_bytes=64)
-    nc.vector.tensor_copy(
-        out=grouped[:, 0, :, :].rearrange("p (g i) j -> p g j i", i=RUN),
-        in_=raw[:, 0, :, :].rearrange("p j (g i) -> p g j i", i=RUN),
-    )
-    nc.scalar.copy(
-        out=grouped[:, 1, :, :].rearrange("p (g i) j -> p g j i", i=RUN),
-        in_=raw[:, 1, :, :].rearrange("p j (g i) -> p g j i", i=RUN),
-    )
+    for c, copy in enumerate((nc.vector.tensor_copy, nc.scalar.copy)):
+        copy(
+            out=grouped[:, c, :, :].rearrange("p (g i) j -> p g j i", i=RUN),
+            in_=raw[:, c, :, :].rearrange("p j (g i) -> p g j i", i=RUN),
+        )
     return grouped
 
 
@@ -127,16 +129,18 @@ def tile_gcn_layer_k_kernel(tc, x, weight, out):
     w_rows = weight.rearrange("one (c p j) o -> p (one c) (j o)", p=P, j=PACK)
     out_view = out.rearrange("b (m o) i j -> b o m (i j)", o=P)
 
+    short = 2 * STEP_PASSES
+    cuts = list(range(0, short, STEP_PASSES)) + list(range(short, PASSES, LOAD_PASSES)) + [PASSES]
     stream = []
-    for s in range(STEPS):
-        stream.append((None, s))
-        stream.append((0, s))
-    for s in range(STEPS):
-        stream.append((1, s))
+    for first, end in zip(cuts, cuts[1:]):
+        stream.append((None, first, end - first))
+        stream.append((0, first, end - first))
+    for first, end in zip(cuts[:0:-1], cuts[-2::-1]):
+        stream.append((1, PASSES - first, first - end))
 
     with tc.tile_pool(name="keep", bufs=1) as keep, tc.tile_pool(
-        name="raw", bufs=12
-    ) as raw_pool, tc.tile_pool(name="grouped", bufs=4) as grouped_pool, tc.tile_pool(
+        name="raw_short", bufs=4
+    ) as raw_short, tc.tile_pool(name="raw_long", bufs=6) as raw_long, tc.tile_pool(name="grouped", bufs=4) as grouped_pool, tc.tile_pool(
         name="x_mx", bufs=4
     ) as x_mx, tc.tile_pool(name="work", bufs=2) as work, tc.psum_pool(
         name="psum", bufs=1
@@ -172,18 +176,20 @@ def tile_gcn_layer_k_kernel(tc, x, weight, out):
                         stop=(k_pass == PASSES - 1),
                     )
 
+        raw_pools = {STEP_PASSES: raw_short, LOAD_PASSES: raw_long}
         regrouped = None
-        for n, (b, s) in enumerate(stream):
-            passes = slice(s * STEP_PASSES, (s + 1) * STEP_PASSES)
-            rows = w_rows[:, passes, :] if b is None else x_rows[b, :, passes, :]
-            grouped = regroup_step(nc, raw_pool, grouped_pool, rows)
-            if regrouped is not None:
-                quantise_and_multiply(*regrouped)
-            regrouped = (grouped, b, s)
-            if b == 1 and s == SUM_AT_STEP:
-                summed_0 = sum_windows(nc, work, psum, graph, 0, acc[0])
-            if b == 1 and s == LEAVE_AT_STEP:
-                result_0 = leave_psum(nc, work, summed_0)
+        for b, first, count in stream:
+            raw = load_passes(nc, raw_pools, w_rows if b is None else x_rows[b], slice(first, first + count))
+            for c in range(0, count, STEP_PASSES):
+                s = (first + c) // STEP_PASSES
+                grouped = regroup_step(nc, grouped_pool, raw[:, c : c + STEP_PASSES, :, :])
+                if regrouped is not None:
+                    quantise_and_multiply(*regrouped)
+                regrouped = (grouped, b, s)
+                if b == 1 and s == SUM_AT_STEP:
+                    summed_0 = sum_windows(nc, work, psum, graph, 0, acc[0])
+                if b == 1 and s == LEAVE_AT_STEP:
+                    result_0 = leave_psum(nc, work, summed_0)
         quantise_and_multiply(*regrouped)
         result_1 = leave_psum(nc, work, sum_windows(nc, work, psum, graph, 1, acc[1]))
 

@@ -1,4 +1,5 @@
 import math
+from contextlib import ExitStack
 
 import concourse.masks as masks
 import concourse.mybir as mybir
@@ -20,19 +21,20 @@ PIXELS = GRID * GRID
 COLS = 256
 PASSES = C_IN // K_PASS
 STEP_PASSES = 2
-LOAD_PASSES = 4
-STEPS = PASSES // STEP_PASSES
+RUN_PASSES = 4
 HALVES = PIXELS // P
 HALF_ROWS = GRID // HALVES
 M_TILES = C_OUT // P
 
 FLOPS = 2 * BATCH * PIXELS * C_IN * C_OUT + 2 * BATCH * PIXELS * PIXELS * C_OUT
 RUN = 4
-SUM_AT_STEP = 2
-LEAVE_AT_STEP = 6
+VECTOR_COLS = 176
+PRODUCT_AT_PASS = 4
+SUM_AT_PASS = 4
+LEAVE_AT_PASS = 12
 
 
-def build_graph(nc, keep):
+def graph_factors(nc, keep):
     one_pixel = keep.tile([P, P], F32)
     masks.make_identity(nc, one_pixel[:])
 
@@ -65,6 +67,10 @@ def build_graph(nc, keep):
     nc.vector.tensor_add(out=factors[:], in0=factors[:], in1=padded[:, :, 2 : GRID + 2])
     nc.vector.tensor_mul(out=factors[:], in0=factors[:], in1=s_all)
 
+    return factors
+
+
+def graph_product(nc, keep, factors):
     graph = keep.tile([P, HALVES, GRID, GRID], F32)
     nc.vector.tensor_mul(
         out=graph[:],
@@ -74,20 +80,35 @@ def build_graph(nc, keep):
     return graph
 
 
-def load_passes(nc, raw_pools, rows, passes):
-    count = passes.stop - passes.start
-    raw = raw_pools[count].tile([P, count, PACK, COLS], BF16, name="raw_%d" % count)
-    nc.sync.dma_start(out=raw[:].rearrange("p c j w -> p c (j w)"), in_=rows[:, passes, :])
+def load_passes(nc, raw_pool, rows, first, count):
+    raw = raw_pool.tile([P, count, PACK, COLS], BF16, name="raw_%d" % count)
+    family = first // RUN_PASSES
+    start = first % RUN_PASSES * PACK * COLS
+    for e in range(2):
+        nc.sync.dma_start(
+            out=raw[e:P:2, :, :, :].rearrange("p c j w -> p (c j w)"),
+            in_=rows[family // 4, family % 4, e, :, start : start + count * PACK * COLS],
+        )
     return raw
 
 
+def interleave(copy, grouped, raw):
+    copy(
+        out=grouped.rearrange("p (g i) j -> p g j i", i=RUN),
+        in_=raw.rearrange("p j (g i) -> p g j i", i=RUN),
+    )
+
+
 def regroup_step(nc, grouped_pool, raw):
-    grouped = grouped_pool.tile([P, STEP_PASSES, COLS, PACK], BF16, align_bytes=64)
-    for c, copy in enumerate((nc.vector.tensor_copy, nc.scalar.copy)):
-        copy(
-            out=grouped[:, c, :, :].rearrange("p (g i) j -> p g j i", i=RUN),
-            in_=raw[:, c, :, :].rearrange("p j (g i) -> p g j i", i=RUN),
-        )
+    count = raw.shape[1]
+    grouped = grouped_pool.tile([P, count, COLS, PACK], BF16, name="grouped_%d" % count, align_bytes=64)
+    if count == 1:
+        split = VECTOR_COLS
+        interleave(nc.vector.tensor_copy, grouped[:, 0, :split, :], raw[:, 0, :, :split])
+        interleave(nc.scalar.copy, grouped[:, 0, split:, :], raw[:, 0, :, split:])
+    else:
+        interleave(nc.vector.tensor_copy, grouped[:, 0, :, :], raw[:, 0, :, :])
+        interleave(nc.scalar.copy, grouped[:, 1, :, :], raw[:, 1, :, :])
     return grouped
 
 
@@ -104,14 +125,21 @@ def sum_windows(nc, work, psum, graph, b, acc):
     nc.vector.tensor_copy(out=xw[:, 0, :], in_=acc[0][:])
     nc.scalar.copy(out=xw[:, 1, :], in_=acc[1][:])
     summed = [psum.tile([P, PIXELS], F32, name="summed_%d_%d" % (b, m)) for m in range(M_TILES)]
+    rows = graph[:].rearrange("p h i j -> p h (i j)")
+    shared = slice(P - GRID, P + GRID)
+    parts = (
+        (0, slice(0, P + GRID), True, False),
+        (1, shared, False, True),
+        (1, slice(P + GRID, PIXELS), True, True),
+    )
     for m in range(M_TILES):
-        for h in range(HALVES):
+        for h, pixels, start, stop in parts:
             nc.tensor.matmul(
-                out=summed[m][:],
+                out=summed[m][:, pixels],
                 lhsT=xw[:, h, m * P : (m + 1) * P],
-                rhs=graph[:, h, :, :].rearrange("p i j -> p (i j)"),
-                start=(h == 0),
-                stop=(h == HALVES - 1),
+                rhs=rows[:, h, pixels],
+                start=start,
+                stop=stop,
             )
     return summed
 
@@ -125,27 +153,42 @@ def leave_psum(nc, work, summed):
 
 def tile_gcn_layer_k_kernel(tc, x, weight, out):
     nc = tc.nc
-    x_rows = x.rearrange("b (c p j) h w -> b p c (j h w)", p=P, j=PACK)
-    w_rows = weight.rearrange("one (c p j) o -> p (one c) (j o)", p=P, j=PACK)
+    x_rows = x.rearrange(
+        "b (half r s e u j) h w -> b half s e r (u j h w)", r=P // 2, s=4, e=2, u=RUN_PASSES, j=PACK
+    )
+    w_rows = weight.rearrange(
+        "one (half r s e u j) o -> (one half) s e r (u j o)", r=P // 2, s=4, e=2, u=RUN_PASSES, j=PACK
+    )
     out_view = out.rearrange("b (m o) i j -> b o m (i j)", o=P)
 
-    short = 2 * STEP_PASSES
-    cuts = list(range(0, short, STEP_PASSES)) + list(range(short, PASSES, LOAD_PASSES)) + [PASSES]
+    head = [1, 1] + [STEP_PASSES] * (PASSES // STEP_PASSES - 1)
+    tail = head[::-1]
     stream = []
-    for first, end in zip(cuts, cuts[1:]):
-        stream.append((None, first, end - first))
-        stream.append((0, first, end - first))
-    for first, end in zip(cuts[:0:-1], cuts[-2::-1]):
-        stream.append((1, PASSES - first, first - end))
+    first = 0
+    for count in head:
+        stream += [(None, first, count), (0, first, count)]
+        first += count
+    first = 0
+    for count in tail:
+        stream.append((1, first, count))
+        first += count
 
-    with tc.tile_pool(name="keep", bufs=1) as keep, tc.tile_pool(
-        name="raw_short", bufs=4
-    ) as raw_short, tc.tile_pool(name="raw_long", bufs=6) as raw_long, tc.tile_pool(name="grouped", bufs=4) as grouped_pool, tc.tile_pool(
-        name="x_mx", bufs=4
-    ) as x_mx, tc.tile_pool(name="work", bufs=2) as work, tc.psum_pool(
-        name="psum", bufs=1
-    ) as psum, tc.manual_schedule():
-        graph = build_graph(nc, keep)
+    with ExitStack() as pools:
+        keep = pools.enter_context(tc.tile_pool(name="keep", bufs=1))
+        raw_pools = {
+            count: pools.enter_context(tc.tile_pool(name="raw_%d" % count, bufs=bufs))
+            for count, bufs in ((1, 6), (STEP_PASSES, 14))
+        }
+        grouped_pool = pools.enter_context(tc.tile_pool(name="grouped", bufs=4))
+        x_mx = pools.enter_context(tc.tile_pool(name="x_mx", bufs=4))
+        work = pools.enter_context(tc.tile_pool(name="work", bufs=2))
+        psum = pools.enter_context(tc.psum_pool(name="psum", bufs=1))
+        pools.enter_context(tc.manual_schedule())
+        blank = keep.tile([P, 2, PACK], F32)
+        nc.vector.memset(blank[:, 0, :], 0.0)
+        nc.scalar.copy(out=blank[:, 1, :], in_=blank[:, 0, :])
+
+        factors = graph_factors(nc, keep)
 
         w_codes = keep.tile([P, PASSES, C_OUT], U32, align_bytes=64)
         w_scales = keep.tile([P, PASSES, C_OUT], U8, align_bytes=64)
@@ -154,16 +197,16 @@ def tile_gcn_layer_k_kernel(tc, x, weight, out):
             for b in range(BATCH)
         ]
 
-        def quantise_and_multiply(grouped, b, s):
-            passes = slice(s * STEP_PASSES, (s + 1) * STEP_PASSES)
+        def quantise_and_multiply(grouped, b, first, count):
+            passes = slice(first, first + count)
             if b is None:
                 quantise(nc, grouped, w_codes[:, passes, :], w_scales[:, passes, :])
                 return
-            x_codes = x_mx.tile([P, STEP_PASSES, PIXELS], U32, align_bytes=64)
-            x_scales = x_mx.tile([P, STEP_PASSES, PIXELS], U8, align_bytes=64)
+            x_codes = x_mx.tile([P, count, PIXELS], U32, name="x_codes_%d" % count, align_bytes=64)
+            x_scales = x_mx.tile([P, count, PIXELS], U8, name="x_scales_%d" % count, align_bytes=64)
             quantise(nc, grouped, x_codes[:], x_scales[:])
-            for c in range(STEP_PASSES):
-                k_pass = s * STEP_PASSES + c
+            for c in range(count):
+                k_pass = first + c
                 for h in range(HALVES):
                     pixels = slice(h * P, (h + 1) * P)
                     nc.tensor.matmul_mx(
@@ -176,20 +219,19 @@ def tile_gcn_layer_k_kernel(tc, x, weight, out):
                         stop=(k_pass == PASSES - 1),
                     )
 
-        raw_pools = {STEP_PASSES: raw_short, LOAD_PASSES: raw_long}
         regrouped = None
         for b, first, count in stream:
-            raw = load_passes(nc, raw_pools, w_rows if b is None else x_rows[b], slice(first, first + count))
-            for c in range(0, count, STEP_PASSES):
-                s = (first + c) // STEP_PASSES
-                grouped = regroup_step(nc, grouped_pool, raw[:, c : c + STEP_PASSES, :, :])
-                if regrouped is not None:
-                    quantise_and_multiply(*regrouped)
-                regrouped = (grouped, b, s)
-                if b == 1 and s == SUM_AT_STEP:
-                    summed_0 = sum_windows(nc, work, psum, graph, 0, acc[0])
-                if b == 1 and s == LEAVE_AT_STEP:
-                    result_0 = leave_psum(nc, work, summed_0)
+            raw = load_passes(nc, raw_pools[count], w_rows if b is None else x_rows[b], first, count)
+            grouped = regroup_step(nc, grouped_pool, raw)
+            if regrouped is not None:
+                quantise_and_multiply(*regrouped)
+            regrouped = (grouped, b, first, count)
+            if b == 0 and first == PRODUCT_AT_PASS:
+                graph = graph_product(nc, keep, factors)
+            if b == 1 and first == SUM_AT_PASS:
+                summed_0 = sum_windows(nc, work, psum, graph, 0, acc[0])
+            if b == 1 and first == LEAVE_AT_PASS:
+                result_0 = leave_psum(nc, work, summed_0)
         quantise_and_multiply(*regrouped)
         result_1 = leave_psum(nc, work, sum_windows(nc, work, psum, graph, 1, acc[1]))
 

@@ -28,10 +28,14 @@ M_TILES = C_OUT // P
 
 FLOPS = 2 * BATCH * PIXELS * C_IN * C_OUT + 2 * BATCH * PIXELS * PIXELS * C_OUT
 RUN = 4
+AHEAD = 3
+TENSOR_FIRST = 14
+TENSOR_EVERY = 3
+TENSOR_PASSES = 10
 VECTOR_COLS = 176
 PRODUCT_AT_PASS = 4
-SUM_AT_PASS = 4
-LEAVE_AT_PASS = 12
+SUM_AT_PASS = 12
+LEAVE_AT_PASS = 20
 
 
 def graph_factors(nc, keep):
@@ -99,16 +103,34 @@ def interleave(copy, grouped, raw):
     )
 
 
-def regroup_step(nc, grouped_pool, raw):
+def regroup_on_tensor(nc, psum, identity, raw, turn):
+    moved = psum.tile([P, COLS, PACK], BF16, name="moved_%d" % turn)
+    for first in range(0, COLS, P):
+        columns = slice(first, first + P)
+        nc.tensor.matmul(
+            out=moved[:, columns, :].rearrange("p w j -> p j w"),
+            lhsT=identity[:],
+            rhs=raw[:, :, columns],
+            start=True,
+            stop=True,
+        )
+    return moved
+
+
+def regroup_step(nc, grouped_pool, raw, moved, scalar_both):
     count = raw.shape[1]
     grouped = grouped_pool.tile([P, count, COLS, PACK], BF16, name="grouped_%d" % count, align_bytes=64)
     if count == 1:
         split = VECTOR_COLS
         interleave(nc.vector.tensor_copy, grouped[:, 0, :split, :], raw[:, 0, :, :split])
         interleave(nc.scalar.copy, grouped[:, 0, split:, :], raw[:, 0, :, split:])
-    else:
-        interleave(nc.vector.tensor_copy, grouped[:, 0, :, :], raw[:, 0, :, :])
+        return grouped
+    if moved is None:
         interleave(nc.scalar.copy, grouped[:, 1, :, :], raw[:, 1, :, :])
+    else:
+        nc.scalar.copy(out=grouped[:, 1, :, :], in_=moved[:])
+    first_copy = nc.scalar.copy if scalar_both else nc.vector.tensor_copy
+    interleave(first_copy, grouped[:, 0, :, :], raw[:, 0, :, :])
     return grouped
 
 
@@ -124,7 +146,7 @@ def sum_windows(nc, work, psum, graph, b, acc):
     xw = work.tile([P, HALVES, C_OUT], F32)
     nc.vector.tensor_copy(out=xw[:, 0, :], in_=acc[0][:])
     nc.scalar.copy(out=xw[:, 1, :], in_=acc[1][:])
-    summed = [psum.tile([P, PIXELS], F32, name="summed_%d_%d" % (b, m)) for m in range(M_TILES)]
+    summed = [psum.tile([P, PIXELS], F32, name="summed_%d" % m) for m in range(M_TILES)]
     rows = graph[:].rearrange("p h i j -> p h (i j)")
     shared = slice(P - GRID, P + GRID)
     parts = (
@@ -161,23 +183,28 @@ def tile_gcn_layer_k_kernel(tc, x, weight, out):
     )
     out_view = out.rearrange("b (m o) i j -> b o m (i j)", o=P)
 
-    head = [1, 1] + [STEP_PASSES] * (PASSES // STEP_PASSES - 1)
-    tail = head[::-1]
-    stream = []
+    head = [1, 1, 2] + [RUN_PASSES] * 7
+    tail = [RUN_PASSES] * 5 + [2] * 5 + [1, 1]
+    loads = []
     first = 0
     for count in head:
-        stream += [(None, first, count), (0, first, count)]
+        loads += [(None, first, count), (0, first, count)]
         first += count
     first = 0
     for count in tail:
-        stream.append((1, first, count))
+        loads.append((1, first, count))
         first += count
+
+    steps = []
+    for load, (b, first, count) in enumerate(loads):
+        for c in range(0, count, STEP_PASSES):
+            steps.append((load, c, min(count, STEP_PASSES)))
 
     with ExitStack() as pools:
         keep = pools.enter_context(tc.tile_pool(name="keep", bufs=1))
         raw_pools = {
             count: pools.enter_context(tc.tile_pool(name="raw_%d" % count, bufs=bufs))
-            for count, bufs in ((1, 6), (STEP_PASSES, 14))
+            for count, bufs in ((1, 6), (STEP_PASSES, 6), (RUN_PASSES, 7))
         }
         grouped_pool = pools.enter_context(tc.tile_pool(name="grouped", bufs=4))
         x_mx = pools.enter_context(tc.tile_pool(name="x_mx", bufs=4))
@@ -189,6 +216,9 @@ def tile_gcn_layer_k_kernel(tc, x, weight, out):
         nc.scalar.copy(out=blank[:, 1, :], in_=blank[:, 0, :])
 
         factors = graph_factors(nc, keep)
+
+        identity = keep.tile([P, P], BF16)
+        masks.make_identity(nc, identity[:])
 
         w_codes = keep.tile([P, PASSES, C_OUT], U32, align_bytes=64)
         w_scales = keep.tile([P, PASSES, C_OUT], U8, align_bytes=64)
@@ -219,10 +249,24 @@ def tile_gcn_layer_k_kernel(tc, x, weight, out):
                         stop=(k_pass == PASSES - 1),
                     )
 
+        raws = []
+        moves = {}
         regrouped = None
-        for b, first, count in stream:
-            raw = load_passes(nc, raw_pools[count], w_rows if b is None else x_rows[b], first, count)
-            grouped = regroup_step(nc, grouped_pool, raw)
+        for n, (load, c, count) in enumerate(steps):
+            ahead = min(n + AHEAD, len(steps) - 1)
+            load_a, c_a, count_a = steps[ahead]
+            while len(raws) <= load_a:
+                b, first, passes = loads[len(raws)]
+                rows = w_rows if b is None else x_rows[b]
+                raws.append(load_passes(nc, raw_pools[passes], rows, first, passes))
+            turn, rest = divmod(ahead - TENSOR_FIRST, TENSOR_EVERY)
+            if rest == 0 and turn in range(TENSOR_PASSES) and ahead not in moves:
+                moves[ahead] = regroup_on_tensor(nc, psum, identity, raws[load_a][:, c_a + 1, :, :], turn % 2)
+            scalar_both = n in moves and (n - TENSOR_FIRST) % (2 * TENSOR_EVERY) == TENSOR_EVERY
+            raw = raws[load][:, c : c + count, :, :]
+            grouped = regroup_step(nc, grouped_pool, raw, moves.get(n), scalar_both)
+            b, first, passes = loads[load]
+            first += c
             if regrouped is not None:
                 quantise_and_multiply(*regrouped)
             regrouped = (grouped, b, first, count)

@@ -29,10 +29,8 @@ M_TILES = C_OUT // P
 FLOPS = 2 * BATCH * PIXELS * C_IN * C_OUT + 2 * BATCH * PIXELS * PIXELS * C_OUT
 RUN = 4
 AHEAD = 3
-TENSOR_FIRST = 14
-TENSOR_EVERY = 3
-TENSOR_PASSES = 10
-VECTOR_COLS = 176
+LONE_VECTOR_COLS = 176
+MOVED_VECTOR_COLS = 152
 PRODUCT_AT_PASS = 4
 SUM_AT_PASS = 12
 LEAVE_AT_PASS = 20
@@ -117,20 +115,21 @@ def regroup_on_tensor(nc, psum, identity, raw, turn):
     return moved
 
 
-def regroup_step(nc, grouped_pool, raw, moved, scalar_both):
+def regroup_step(nc, grouped_pool, raw, moved):
     count = raw.shape[1]
     grouped = grouped_pool.tile([P, count, COLS, PACK], BF16, name="grouped_%d" % count, align_bytes=64)
+    split = COLS
     if count == 1:
-        split = VECTOR_COLS
-        interleave(nc.vector.tensor_copy, grouped[:, 0, :split, :], raw[:, 0, :, :split])
+        split = LONE_VECTOR_COLS
+    elif moved is not None:
+        split = MOVED_VECTOR_COLS
+    interleave(nc.vector.tensor_copy, grouped[:, 0, :split, :], raw[:, 0, :, :split])
+    if split < COLS:
         interleave(nc.scalar.copy, grouped[:, 0, split:, :], raw[:, 0, :, split:])
-        return grouped
-    if moved is None:
-        interleave(nc.scalar.copy, grouped[:, 1, :, :], raw[:, 1, :, :])
-    else:
+    if moved is not None:
         nc.scalar.copy(out=grouped[:, 1, :, :], in_=moved[:])
-    first_copy = nc.scalar.copy if scalar_both else nc.vector.tensor_copy
-    interleave(first_copy, grouped[:, 0, :, :], raw[:, 0, :, :])
+    elif count == 2:
+        interleave(nc.scalar.copy, grouped[:, 1, :, :], raw[:, 1, :, :])
     return grouped
 
 
@@ -142,10 +141,10 @@ def quantise(nc, grouped, codes, scales):
     )
 
 
-def sum_windows(nc, work, psum, graph, b, acc):
+def sum_windows(nc, work, psum, graph, acc, copies):
     xw = work.tile([P, HALVES, C_OUT], F32)
-    nc.vector.tensor_copy(out=xw[:, 0, :], in_=acc[0][:])
-    nc.scalar.copy(out=xw[:, 1, :], in_=acc[1][:])
+    for h, copy in enumerate(copies):
+        copy(out=xw[:, h, :], in_=acc[h][:])
     summed = [psum.tile([P, PIXELS], F32, name="summed_%d" % m) for m in range(M_TILES)]
     rows = graph[:].rearrange("p h i j -> p h (i j)")
     shared = slice(P - GRID, P + GRID)
@@ -166,10 +165,10 @@ def sum_windows(nc, work, psum, graph, b, acc):
     return summed
 
 
-def leave_psum(nc, work, summed):
+def leave_psum(work, summed, copies):
     result = work.tile([P, M_TILES, PIXELS], F32)
-    nc.vector.tensor_copy(out=result[:, 0, :], in_=summed[0][:])
-    nc.scalar.copy(out=result[:, 1, :], in_=summed[1][:])
+    for m, copy in enumerate(copies):
+        copy(out=result[:, m, :], in_=summed[m][:])
     return result
 
 
@@ -199,6 +198,8 @@ def tile_gcn_layer_k_kernel(tc, x, weight, out):
     for load, (b, first, count) in enumerate(loads):
         for c in range(0, count, STEP_PASSES):
             steps.append((load, c, min(count, STEP_PASSES)))
+    ends = [n for n, (load, c, count) in enumerate(steps) if c + count == RUN_PASSES]
+    tensor_steps = ends[1::2]
 
     with ExitStack() as pools:
         keep = pools.enter_context(tc.tile_pool(name="keep", bufs=1))
@@ -249,6 +250,8 @@ def tile_gcn_layer_k_kernel(tc, x, weight, out):
                         stop=(k_pass == PASSES - 1),
                     )
 
+        both = (nc.vector.tensor_copy, nc.scalar.copy)
+        scalar_alone = (nc.scalar.copy, nc.scalar.copy)
         raws = []
         moves = {}
         regrouped = None
@@ -259,12 +262,11 @@ def tile_gcn_layer_k_kernel(tc, x, weight, out):
                 b, first, passes = loads[len(raws)]
                 rows = w_rows if b is None else x_rows[b]
                 raws.append(load_passes(nc, raw_pools[passes], rows, first, passes))
-            turn, rest = divmod(ahead - TENSOR_FIRST, TENSOR_EVERY)
-            if rest == 0 and turn in range(TENSOR_PASSES) and ahead not in moves:
-                moves[ahead] = regroup_on_tensor(nc, psum, identity, raws[load_a][:, c_a + 1, :, :], turn % 2)
-            scalar_both = n in moves and (n - TENSOR_FIRST) % (2 * TENSOR_EVERY) == TENSOR_EVERY
+            if ahead in tensor_steps and ahead not in moves:
+                last = raws[load_a][:, RUN_PASSES - 1, :, :]
+                moves[ahead] = regroup_on_tensor(nc, psum, identity, last, len(moves) % 2)
             raw = raws[load][:, c : c + count, :, :]
-            grouped = regroup_step(nc, grouped_pool, raw, moves.get(n), scalar_both)
+            grouped = regroup_step(nc, grouped_pool, raw, moves.get(n))
             b, first, passes = loads[load]
             first += c
             if regrouped is not None:
@@ -273,11 +275,12 @@ def tile_gcn_layer_k_kernel(tc, x, weight, out):
             if b == 0 and first == PRODUCT_AT_PASS:
                 graph = graph_product(nc, keep, factors)
             if b == 1 and first == SUM_AT_PASS:
-                summed_0 = sum_windows(nc, work, psum, graph, 0, acc[0])
+                summed_0 = sum_windows(nc, work, psum, graph, acc[0], scalar_alone)
             if b == 1 and first == LEAVE_AT_PASS:
-                result_0 = leave_psum(nc, work, summed_0)
+                result_0 = leave_psum(work, summed_0, scalar_alone)
         quantise_and_multiply(*regrouped)
-        result_1 = leave_psum(nc, work, sum_windows(nc, work, psum, graph, 1, acc[1]))
+        summed_1 = sum_windows(nc, work, psum, graph, acc[1], both)
+        result_1 = leave_psum(work, summed_1, both)
 
         for b, result in enumerate((result_0, result_1)):
             for m in range(M_TILES):

@@ -29,7 +29,7 @@ M_TILES = C_OUT // P
 FLOPS = 2 * BATCH * PIXELS * C_IN * C_OUT + 2 * BATCH * PIXELS * PIXELS * C_OUT
 RUN = 4
 AHEAD = 3
-LONE_VECTOR_COLS = 176
+LONE_VECTOR_COLS = 152
 MOVED_VECTOR_COLS = 152
 PRODUCT_AT_PASS = 4
 SUM_AT_PASS = 12
@@ -143,8 +143,9 @@ def quantise(nc, grouped, codes, scales):
 
 def sum_windows(nc, work, psum, graph, acc, copies):
     xw = work.tile([P, HALVES, C_OUT], F32)
-    for h, copy in enumerate(copies):
-        copy(out=xw[:, h, :], in_=acc[h][:])
+    for m in range(M_TILES):
+        for h, copy in enumerate(copies):
+            copy(out=xw[:, h, m * P : (m + 1) * P], in_=acc[h][:, m * P : (m + 1) * P])
     summed = [psum.tile([P, PIXELS], F32, name="summed_%d" % m) for m in range(M_TILES)]
     rows = graph[:].rearrange("p h i j -> p h (i j)")
     shared = slice(P - GRID, P + GRID)
@@ -182,7 +183,7 @@ def tile_gcn_layer_k_kernel(tc, x, weight, out):
     )
     out_view = out.rearrange("b (m o) i j -> b o m (i j)", o=P)
 
-    head = [1, 1, 2] + [RUN_PASSES] * 7
+    head = [1, 1, 2, 2, 2] + [RUN_PASSES] * 6
     tail = [RUN_PASSES] * 5 + [2] * 5 + [1, 1]
     loads = []
     first = 0

import math
from contextlib import ExitStack

import concourse.masks as masks
import concourse.mybir as mybir

BF16 = mybir.dt.bfloat16
F32 = mybir.dt.float32
U32 = mybir.dt.uint32
U8 = mybir.dt.uint8
FP8X4 = mybir.dt.float8_e4m3fn_x4

P = 128
PACK = 4
K_PASS = P * PACK
BATCH = 2
C_IN = 16384
C_OUT = 256
GRID = 16
PIXELS = GRID * GRID
COLS = 256
PASSES = C_IN // K_PASS
STEP_PASSES = 2
RUN_PASSES = 4
HALVES = PIXELS // P
HALF_ROWS = GRID // HALVES
M_TILES = C_OUT // P

FLOPS = 2 * BATCH * PIXELS * C_IN * C_OUT + 2 * BATCH * PIXELS * PIXELS * C_OUT
RUN = 4
AHEAD = 3
LONE_VECTOR_COLS = 152
MOVED_VECTOR_COLS = 152
PRODUCT_AT_PASS = 4
SUM_AT_PASS = 12
LEAVE_AT_PASS = 20


def graph_factors(nc, keep):
    one_pixel = keep.tile([P, P], F32)
    masks.make_identity(nc, one_pixel[:])

    s = keep.tile([P, GRID], F32)
    nc.vector.memset(s[:], 1.0)
    nc.vector.tensor_scalar_mul(out=s[:], in0=s[:], scalar1=1.0 / math.sqrt(3.0))
    ends = s[:, 0 : GRID : GRID - 1]
    nc.vector.tensor_scalar_mul(out=ends, in0=ends, scalar1=math.sqrt(1.5))
    s_all = s[:].unsqueeze(1).to_broadcast([P, 1 + HALVES, GRID])

    padded = keep.tile([P, 1 + HALVES, GRID + 2], F32)
    nc.vector.memset(padded[:], 0.0)
    nc.vector.tensor_reduce(
        out=padded[:, 0, 1 : GRID + 1],
        in_=one_pixel[:].rearrange("p (i j) -> p j i", j=GRID),
        axis=mybir.AxisListType.X,
        op=mybir.AluOpType.add,
    )
    for h in range(HALVES):
        nc.vector.tensor_reduce(
            out=padded[:, 1 + h, 1 + h * HALF_ROWS : 1 + (h + 1) * HALF_ROWS],
            in_=one_pixel[:].rearrange("p (i j) -> p i j", j=GRID),
            axis=mybir.AxisListType.X,
            op=mybir.AluOpType.add,
        )
    centre = padded[:, :, 1 : GRID + 1]
    nc.vector.tensor_mul(out=centre, in0=centre, in1=s_all)
    factors = keep.tile([P, 1 + HALVES, GRID], F32)
    nc.vector.tensor_add(out=factors[:], in0=padded[:, :, 0:GRID], in1=centre)
    nc.vector.tensor_add(out=factors[:], in0=factors[:], in1=padded[:, :, 2 : GRID + 2])
    nc.vector.tensor_mul(out=factors[:], in0=factors[:], in1=s_all)

    return factors


def graph_product(nc, keep, factors):
    graph = keep.tile([P, HALVES, GRID, GRID], F32)
    nc.vector.tensor_mul(
        out=graph[:],
        in0=factors[:, 1 : 1 + HALVES, :].unsqueeze(3).to_broadcast([P, HALVES, GRID, GRID]),
        in1=factors[:, 0:1, :].unsqueeze(1).to_broadcast([P, HALVES, GRID, GRID]),
    )
    return graph


def load_passes(nc, raw_pool, rows, first, count):
    raw = raw_pool.tile([P, count, PACK, COLS], BF16, name="raw_%d" % count)
    family = first // RUN_PASSES
    start = first % RUN_PASSES * PACK * COLS
    for e in range(2):
        nc.sync.dma_start(
            out=raw[e:P:2, :, :, :].rearrange("p c j w -> p (c j w)"),
            in_=rows[family // 4, family % 4, e, :, start : start + count * PACK * COLS],
        )
    return raw


def interleave(copy, grouped, raw):
    copy(
        out=grouped.rearrange("p (g i) j -> p g j i", i=RUN),
        in_=raw.rearrange("p j (g i) -> p g j i", i=RUN),
    )


def regroup_on_tensor(nc, psum, identity, raw, turn):
    moved = psum.tile([P, COLS, PACK], BF16, name="moved_%d" % turn)
    for first in range(0, COLS, P):
        columns = slice(first, first + P)
        nc.tensor.matmul(
            out=moved[:, columns, :].rearrange("p w j -> p j w"),
            lhsT=identity[:],
            rhs=raw[:, :, columns],
            start=True,
            stop=True,
        )
    return moved


def regroup_step(nc, grouped_pool, raw, moved):
    count = raw.shape[1]
    grouped = grouped_pool.tile([P, count, COLS, PACK], BF16, name="grouped_%d" % count, align_bytes=64)
    split = COLS
    if count == 1:
        split = LONE_VECTOR_COLS
    elif moved is not None:
        split = MOVED_VECTOR_COLS
    interleave(nc.vector.tensor_copy, grouped[:, 0, :split, :], raw[:, 0, :, :split])
    if split < COLS:
        interleave(nc.scalar.copy, grouped[:, 0, split:, :], raw[:, 0, :, split:])
    if moved is not None:
        nc.scalar.copy(out=grouped[:, 1, :, :], in_=moved[:])
    elif count == 2:
        interleave(nc.scalar.copy, grouped[:, 1, :, :], raw[:, 1, :, :])
    return grouped


def quantise(nc, grouped, codes, scales):
    nc.vector.quantize_mx(
        out=codes.rearrange("p c w -> p (c w)").bitcast(FP8X4),
        scales=scales.rearrange("p c w -> p (c w)"),
        in_=grouped[:].rearrange("p c w j -> p (c w j)"),
    )


def sum_windows(nc, work, psum, graph, acc, copies):
    xw = work.tile([P, HALVES, C_OUT], F32)
    for m in range(M_TILES):
        for h, copy in enumerate(copies):
            copy(out=xw[:, h, m * P : (m + 1) * P], in_=acc[h][:, m * P : (m + 1) * P])
    summed = [psum.tile([P, PIXELS], F32, name="summed_%d" % m) for m in range(M_TILES)]
    rows = graph[:].rearrange("p h i j -> p h (i j)")
    shared = slice(P - GRID, P + GRID)
    parts = (
        (0, slice(0, P + GRID), True, False),
        (1, shared, False, True),
        (1, slice(P + GRID, PIXELS), True, True),
    )
    for m in range(M_TILES):
        for h, pixels, start, stop in parts:
            nc.tensor.matmul(
                out=summed[m][:, pixels],
                lhsT=xw[:, h, m * P : (m + 1) * P],
                rhs=rows[:, h, pixels],
                start=start,
                stop=stop,
            )
    return summed


def leave_psum(work, summed, copies):
    result = work.tile([P, M_TILES, PIXELS], F32)
    for m, copy in enumerate(copies):
        copy(out=result[:, m, :], in_=summed[m][:])
    return result


def tile_gcn_layer_k_kernel(tc, x, weight, out):
    nc = tc.nc
    x_rows = x.rearrange(
        "b (half r s e u j) h w -> b half s e r (u j h w)", r=P // 2, s=4, e=2, u=RUN_PASSES, j=PACK
    )
    w_rows = weight.rearrange(
        "one (half r s e u j) o -> (one half) s e r (u j o)", r=P // 2, s=4, e=2, u=RUN_PASSES, j=PACK
    )
    out_view = out.rearrange("b (m o) i j -> b o m (i j)", o=P)

    head = [1, 1, 2, 2, 2] + [RUN_PASSES] * 6
    tail = [RUN_PASSES] * 5 + [2] * 5 + [1, 1]
    loads = []
    first = 0
    for count in head:
        loads += [(None, first, count), (0, first, count)]
        first += count
    first = 0
    for count in tail:
        loads.append((1, first, count))
        first += count

    steps = []
    for load, (b, first, count) in enumerate(loads):
        for c in range(0, count, STEP_PASSES):
            steps.append((load, c, min(count, STEP_PASSES)))
    ends = [n for n, (load, c, count) in enumerate(steps) if c + count == RUN_PASSES]
    tensor_steps = ends[1::2]

    with ExitStack() as pools:
        keep = pools.enter_context(tc.tile_pool(name="keep", bufs=1))
        raw_pools = {
            count: pools.enter_context(tc.tile_pool(name="raw_%d" % count, bufs=bufs))
            for count, bufs in ((1, 6), (STEP_PASSES, 6), (RUN_PASSES, 7))
        }
        grouped_pool = pools.enter_context(tc.tile_pool(name="grouped", bufs=4))
        x_mx = pools.enter_context(tc.tile_pool(name="x_mx", bufs=4))
        work = pools.enter_context(tc.tile_pool(name="work", bufs=2))
        psum = pools.enter_context(tc.psum_pool(name="psum", bufs=1))
        pools.enter_context(tc.manual_schedule())
        blank = keep.tile([P, 2, PACK], F32)
        nc.vector.memset(blank[:, 0, :], 0.0)
        nc.scalar.copy(out=blank[:, 1, :], in_=blank[:, 0, :])

        factors = graph_factors(nc, keep)

        identity = keep.tile([P, P], BF16)
        masks.make_identity(nc, identity[:])

        w_codes = keep.tile([P, PASSES, C_OUT], U32, align_bytes=64)
        w_scales = keep.tile([P, PASSES, C_OUT], U8, align_bytes=64)
        acc = [
            [psum.tile([P, C_OUT], F32, name="acc_%d_%d" % (b, h)) for h in range(HALVES)]
            for b in range(BATCH)
        ]

        def quantise_and_multiply(grouped, b, first, count):
            passes = slice(first, first + count)
            if b is None:
                quantise(nc, grouped, w_codes[:, passes, :], w_scales[:, passes, :])
                return
            x_codes = x_mx.tile([P, count, PIXELS], U32, name="x_codes_%d" % count, align_bytes=64)
            x_scales = x_mx.tile([P, count, PIXELS], U8, name="x_scales_%d" % count, align_bytes=64)
            quantise(nc, grouped, x_codes[:], x_scales[:])
            for c in range(count):
                k_pass = first + c
                for h in range(HALVES):
                    pixels = slice(h * P, (h + 1) * P)
                    nc.tensor.matmul_mx(
                        out=acc[b][h][:],
                        lhsT=x_codes[:, c, pixels].bitcast(FP8X4),
                        lhsT_scale=x_scales[:, c, pixels],
                        rhs=w_codes[:, k_pass, :].bitcast(FP8X4),
                        rhs_scale=w_scales[:, k_pass, :],
                        start=(k_pass == 0),
                        stop=(k_pass == PASSES - 1),
                    )

        both = (nc.vector.tensor_copy, nc.scalar.copy)
        scalar_alone = (nc.scalar.copy, nc.scalar.copy)
        raws = []
        moves = {}
        regrouped = None
        for n, (load, c, count) in enumerate(steps):
            ahead = min(n + AHEAD, len(steps) - 1)
            load_a, c_a, count_a = steps[ahead]
            while len(raws) <= load_a:
                b, first, passes = loads[len(raws)]
                rows = w_rows if b is None else x_rows[b]
                raws.append(load_passes(nc, raw_pools[passes], rows, first, passes))
            if ahead in tensor_steps and ahead not in moves:
                last = raws[load_a][:, RUN_PASSES - 1, :, :]
                moves[ahead] = regroup_on_tensor(nc, psum, identity, last, len(moves) % 2)
            raw = raws[load][:, c : c + count, :, :]
            grouped = regroup_step(nc, grouped_pool, raw, moves.get(n))
            b, first, passes = loads[load]
            first += c
            if regrouped is not None:
                quantise_and_multiply(*regrouped)
            regrouped = (grouped, b, first, count)
            if b == 0 and first == PRODUCT_AT_PASS:
                graph = graph_product(nc, keep, factors)
            if b == 1 and first == SUM_AT_PASS:
                summed_0 = sum_windows(nc, work, psum, graph, acc[0], scalar_alone)
            if b == 1 and first == LEAVE_AT_PASS:
                result_0 = leave_psum(work, summed_0, scalar_alone)
        quantise_and_multiply(*regrouped)
        summed_1 = sum_windows(nc, work, psum, graph, acc[1], both)
        result_1 = leave_psum(work, summed_1, both)

        for b, result in enumerate((result_0, result_1)):
            for m in range(M_TILES):
                nc.sync.dma_start(out=out_view[b, :, m, :], in_=result[:, m, :])
